import numpy as np
import ml_dtypes


def mxq(x, axis, fmt="e4m3"):
    dtype, down = {"e4m3": (ml_dtypes.float8_e4m3fn, 7), "e5m2": (ml_dtypes.float8_e5m2, 14)}[fmt]
    v = np.moveaxis(np.asarray(x, np.float32).astype(ml_dtypes.bfloat16).astype(np.float64), axis, -1)
    blocks = v.reshape(v.shape[:-1] + (-1, 32))
    amax = np.abs(blocks).max(-1, keepdims=True)
    byte = np.maximum(np.where(amax > 0, np.frexp(amax)[1] - 1 + 127, 0) - down, 1)
    scale = np.exp2(byte - 127.0)
    codes = (blocks / scale).astype(np.float32).astype(dtype).astype(np.float64)
    return np.moveaxis((codes * scale).reshape(v.shape), -1, axis)


WIDE = False


def mx_kscale(k):
    if not WIDE:
        return np.ones(k)
    levels = np.array([10, -10, 5, -5, 0])
    a = np.random.permutation(np.resize(levels, k // 512 * 4)).reshape(k // 512, 4)
    idx = np.arange(k)
    return np.exp2(a[idx // 512, idx % 128 // 32])


BF16 = ml_dtypes.bfloat16


def bf(x):
    return np.asarray(x, np.float32).astype(BF16)


def f64(x):
    return np.asarray(x).astype(np.float64)


B, A, G, H1, H2 = 256, 128, 5, 16384, 512
SLOPE = 0.4


def leaky(v):
    return np.where(v >= 0.0, v, SLOPE * v)


def setup_inputs():
    s, t = mx_kscale(H1), mx_kscale(H2)
    keep = np.where(np.random.uniform(size=(B, A)) > 0.2, 1.0, 0.0)
    return {"x": bf(np.random.standard_normal((B, A * G)) * np.repeat(keep, G, axis=1)),
            "h1": bf(leaky(np.random.standard_normal((B, H1))) * s),
            "W2": bf(np.random.standard_normal((H1, H2)) * 1.3 / np.sqrt(H1) / s[:, None] * t),
            "b2": bf(np.random.standard_normal(H2) * 0.3 * t),
            "W3": bf(np.random.standard_normal((H2, A)) * 2.5 / np.sqrt(H2) / t[:, None]),
            "b3": bf(np.random.standard_normal(A) * 0.5)}


def reference(x, h1, W2, b2, W3, b3):
    gsum = f64(x).reshape(B, A, G).sum(axis=-1)
    mask = gsum != 0.0
    h2 = leaky((mxq(f64(h1), 1, "e4m3") @ mxq(f64(W2), 0, "e4m3")) + f64(b2))
    logits = (mxq(h2, 1, "e4m3") @ mxq(f64(W3), 0, "e4m3")) + f64(b3)
    logits = np.where(mask, logits, -np.inf)
    e = np.exp(logits - logits.max(axis=1, keepdims=True))
    return e / e.sum(axis=1, keepdims=True)

@@ -1,0 +1,276 @@
+from contextlib import ExitStack
+
+import concourse.mybir as mybir
+from concourse.masks import make_identity
+
+F32 = mybir.dt.float32
+BF16 = mybir.dt.bfloat16
+U32 = mybir.dt.uint32
+U8 = mybir.dt.uint8
+FP8X4 = mybir.dt.float8_e4m3fn_x4
+ALU = mybir.AluOpType
+ACT = mybir.ActivationFunctionType
+AX = mybir.AxisListType
+
+B, A, G, H1, H2 = 256, 128, 5, 16384, 512
+SLOPE = 0.4
+FLOPS = 2 * B * H1 * H2 + 2 * B * H2 * A
+
+P = 128
+PACK = 4
+K_PASS = P * PACK
+PASSES = H1 // K_PASS
+ROW_TILES = B // P
+H2_TILES = H2 // P
+
+PERIOD_PASSES = 4
+PERIODS = PASSES // PERIOD_PASSES
+PERIOD_K = PERIOD_PASSES * K_PASS
+W2_LOAD_PASSES = 2
+W2_LOADS = PASSES // W2_LOAD_PASSES
+H1_LEAD = 1
+VECTOR_COLS = 288
+MASKED = -3.0e38
+
+
+def tile_dqn_pa_k_kernel(tc, x, h1, W2, b2, W3, b3, out):
+    nc = tc.nc
+    with ExitStack() as ctx:
+        const = ctx.enter_context(tc.tile_pool(name="const", bufs=1))
+        h_raw_pool = ctx.enter_context(tc.tile_pool(name="h_raw", bufs=3))
+        h_grp_pool = ctx.enter_context(tc.tile_pool(name="h_grp", bufs=2))
+        w_raw_pool = ctx.enter_context(tc.tile_pool(name="w_raw", bufs=6))
+        w_grp_pool = ctx.enter_context(tc.tile_pool(name="w_grp", bufs=4))
+        w_mx_pool = ctx.enter_context(tc.tile_pool(name="w_mx", bufs=4))
+        soft = ctx.enter_context(tc.tile_pool(name="soft", bufs=2))
+        acc_pool = ctx.enter_context(tc.psum_pool(name="acc", bufs=1))
+        bank_pool = ctx.enter_context(tc.psum_pool(name="bank", bufs=4))
+
+        def load_h1(c):
+            raw = h_raw_pool.tile([P, ROW_TILES * PERIOD_K], BF16, name="h_raw")
+            nc.sync.dma_start(
+                out=raw[:].rearrange("p (r k) -> p r k", r=ROW_TILES),
+                in_=h1[:, c * PERIOD_K : (c + 1) * PERIOD_K].rearrange("(r p) k -> p r k", p=P),
+            )
+            return raw
+
+        def load_w2(c):
+            raw = w_raw_pool.tile([P, W2_LOAD_PASSES, PACK, H2], BF16, name="w_raw")
+            rows = W2[c * W2_LOAD_PASSES * K_PASS : (c + 1) * W2_LOAD_PASSES * K_PASS, :]
+            nc.sync.dma_start(
+                out=raw[:].rearrange("p g (u e) n -> p (g u) (e n)", u=2),
+                in_=rows.rearrange("(g u p e) n -> p (g u) (e n)", g=W2_LOAD_PASSES, u=2, p=P),
+            )
+            return raw
+
+        h_raw = {}
+        w_raw = {}
+        for c in range(H1_LEAD):
+            h_raw[c] = load_h1(c)
+        for i in range(PERIODS):
+            if i + H1_LEAD < PERIODS:
+                h_raw[i + H1_LEAD] = load_h1(i + H1_LEAD)
+            for c in range(i * W2_LOADS // PERIODS, (i + 1) * W2_LOADS // PERIODS):
+                w_raw[c] = load_w2(c)
+
+        x_sb = const.tile([P, ROW_TILES, A * G], BF16)
+        nc.scalar.dma_start(out=x_sb[:], in_=x.rearrange("(r p) c -> p r c", p=P))
+        w3_raw = const.tile([P, PACK, A], BF16)
+        nc.scalar.dma_start(out=w3_raw[:], in_=W3.rearrange("(t p) a -> p t a", p=P))
+        b3_all = const.tile([P, A], BF16)
+        nc.scalar.dma_start(out=b3_all[:], in_=b3.partition_broadcast(P))
+        b2_rows = const.tile([H2_TILES, P], BF16)
+        nc.scalar.dma_start(out=b2_rows[:], in_=b2.rearrange("(j p) -> j p", p=P))
+
+        ident = const.tile([P, P], F32)
+        make_identity(nc, ident[:])
+
+        zero_col = const.tile([P, 1], F32)
+        nc.vector.memset(zero_col[:], 0.0)
+        one_col = const.tile([P, 1], F32)
+        nc.scalar.activation(out=one_col[:], in_=zero_col[:], func=ACT.Exp)
+
+        b2_square = const.tile([P, P], F32)
+        nc.vector.memset(b2_square[:], 0.0)
+        nc.vector.tensor_copy(out=b2_square[0:H2_TILES, :], in_=b2_rows[:])
+        b2_bank = bank_pool.tile([P, P], F32, tag="bank")
+        nc.tensor.transpose(b2_bank[:], b2_square[:], ident[:])
+        b2_col = const.tile([P, H2_TILES], F32)
+        nc.vector.tensor_copy(out=b2_col[:], in_=b2_bank[:, 0:H2_TILES])
+
+        gsum = const.tile([P, ROW_TILES, A], F32)
+        nc.vector.tensor_reduce(
+            out=gsum[:], in_=x_sb[:].rearrange("p r (a g) -> p r a g", g=G), axis=AX.X, op=ALU.add
+        )
+        bias_mask = const.tile([P, ROW_TILES, A], F32)
+        nc.vector.tensor_scalar(
+            out=bias_mask[:], in0=gsum[:], scalar1=0.0, scalar2=MASKED, op0=ALU.is_equal, op1=ALU.mult
+        )
+        for r in range(ROW_TILES):
+            nc.vector.tensor_tensor(
+                out=bias_mask[:, r, :], in0=bias_mask[:, r, :], in1=b3_all[:], op=ALU.add
+            )
+
+        w3_grp = const.tile([P, A, PACK], BF16, align_bytes=64)
+        nc.vector.tensor_copy(out=w3_grp[:], in_=w3_raw[:].rearrange("p t a -> p a t"))
+        w3_codes = const.tile([P, A], U32, align_bytes=64)
+        w3_scale = const.tile([P, A], U8, align_bytes=64)
+        nc.vector.quantize_mx(
+            out=w3_codes[:].bitcast(FP8X4),
+            scales=w3_scale[:],
+            in_=w3_grp[:].rearrange("p a t -> p (a t)"),
+        )
+
+        h_codes = const.tile([P, PASSES * B], U32, align_bytes=64)
+        h_scale = const.tile([P, PASSES * B], U8, align_bytes=64)
+        acc = [acc_pool.tile([P, B], F32, name="acc%d" % j) for j in range(H2_TILES)]
+
+        def transpose_h1(c):
+            words = h_raw[c][:].bitcast(F32)
+            banks = []
+            for g in range(PERIOD_PASSES):
+                bank = bank_pool.tile([P, 2, B], F32, tag="bank", name="h_bank")
+                for u in range(2):
+                    for r in range(ROW_TILES):
+                        first = r * PERIOD_K // 2 + (2 * g + u) * P
+                        nc.tensor.transpose(
+                            bank[:, u, r * P : (r + 1) * P], words[:, first : first + P], ident[:]
+                        )
+                banks.append(bank)
+            return banks
+
+        def copy_h1(grp, g, bank):
+            pairs = grp[:].bitcast(F32)[:, g * 2 * B : (g + 1) * 2 * B]
+            nc.scalar.copy(
+                out=pairs.rearrange("p (i u) -> p i u", u=2), in_=bank[:].rearrange("p u i -> p i u")
+            )
+
+        def quantise_h1(c, grp):
+            cols = slice(c * PERIOD_PASSES * B, (c + 1) * PERIOD_PASSES * B)
+            nc.vector.quantize_mx(
+                out=h_codes[:, cols].bitcast(FP8X4), scales=h_scale[:, cols], in_=grp[:]
+            )
+
+        def regroup_w2(g):
+            rows = w_raw[g // W2_LOAD_PASSES][:, g % W2_LOAD_PASSES]
+            grp = w_grp_pool.tile([P, H2, PACK], BF16, align_bytes=64, name="w_grp")
+            nc.vector.tensor_copy(
+                out=grp[:, 0:VECTOR_COLS, :].rearrange("p (c i) t -> p c t i", i=4),
+                in_=rows[:, :, 0:VECTOR_COLS].rearrange("p t (c i) -> p c t i", i=4),
+            )
+            nc.scalar.copy(
+                out=grp[:, VECTOR_COLS:H2, :].rearrange("p (c i) t -> p c t i", i=4),
+                in_=rows[:, :, VECTOR_COLS:H2].rearrange("p t (c i) -> p c t i", i=4),
+            )
+            return grp
+
+        def quantise_w2(grp):
+            codes = w_mx_pool.tile([P, H2], U32, align_bytes=64, name="w_codes")
+            scale = w_mx_pool.tile([P, H2], U8, align_bytes=64, name="w_scale")
+            nc.vector.quantize_mx(
+                out=codes[:].bitcast(FP8X4), scales=scale[:], in_=grp[:].rearrange("p n t -> p (n t)")
+            )
+            return codes, scale
+
+        def multiply(g, codes, scale):
+            rows = slice(g * B, (g + 1) * B)
+            for j in range(H2_TILES):
+                cols = slice(j * P, (j + 1) * P)
+                nc.tensor.matmul_mx(
+                    out=acc[j][:],
+                    lhsT=codes[:, cols].bitcast(FP8X4),
+                    lhsT_scale=scale[:, cols],
+                    rhs=h_codes[:, rows].bitcast(FP8X4),
+                    rhs_scale=h_scale[:, rows],
+                    start=(g == 0),
+                    stop=(g == PASSES - 1),
+                )
+
+        for c in range(H1_LEAD):
+            banks = transpose_h1(c)
+            h_grp = h_grp_pool.tile([P, PERIOD_PASSES * B * PACK], BF16, align_bytes=64, name="h_grp")
+            for g in range(PERIOD_PASSES):
+                copy_h1(h_grp, g, banks[g])
+            quantise_h1(c, h_grp)
+
+        w_grp = {}
+        w_mx = {}
+        for i in range(PERIODS):
+            c = i + H1_LEAD
+            if c < PERIODS:
+                banks = transpose_h1(c)
+                h_grp = h_grp_pool.tile(
+                    [P, PERIOD_PASSES * B * PACK], BF16, align_bytes=64, name="h_grp"
+                )
+            for s in range(PERIOD_PASSES):
+                g = i * PERIOD_PASSES + s
+                if c < PERIODS:
+                    copy_h1(h_grp, s, banks[s])
+                w_grp[g] = regroup_w2(g)
+                if g >= 1:
+                    w_mx[g - 1] = quantise_w2(w_grp[g - 1])
+                if g >= 2:
+                    multiply(g - 2, w_mx[g - 2][0], w_mx[g - 2][1])
+            if c < PERIODS:
+                quantise_h1(c, h_grp)
+        w_mx[PASSES - 1] = quantise_w2(w_grp[PASSES - 1])
+        multiply(PASSES - 2, w_mx[PASSES - 2][0], w_mx[PASSES - 2][1])
+        multiply(PASSES - 1, w_mx[PASSES - 1][0], w_mx[PASSES - 1][1])
+
+        pre = const.tile([P, H2_TILES, B], F32)
+        for j in range(H2_TILES):
+            if j % 2 == 0:
+                nc.vector.tensor_scalar(
+                    out=pre[:, j, :], in0=acc[j][:], scalar1=b2_col[:, j : j + 1], scalar2=None, op0=ALU.add
+                )
+            else:
+                nc.scalar.activation(
+                    out=pre[:, j, :], in_=acc[j][:], func=ACT.Identity, bias=b2_col[:, j : j + 1], scale=1.0
+                )
+        h2_grp = const.tile([P, B, PACK], BF16, align_bytes=64)
+        h2_codes = const.tile([P, B], U32, align_bytes=64)
+        h2_scale = const.tile([P, B], U8, align_bytes=64)
+        for r in range(ROW_TILES):
+            rows = slice(r * P, (r + 1) * P)
+            turned = pre[:, :, rows].rearrange("p t i -> p i t")
+            nc.vector.scalar_tensor_tensor(
+                out=h2_grp[:, rows, :], in0=turned, scalar=SLOPE, in1=turned, op0=ALU.mult, op1=ALU.max
+            )
+        for r in range(ROW_TILES):
+            rows = slice(r * P, (r + 1) * P)
+            nc.vector.quantize_mx(
+                out=h2_codes[:, rows].bitcast(FP8X4),
+                scales=h2_scale[:, rows],
+                in_=h2_grp[:, rows, :].rearrange("p i t -> p (i t)"),
+            )
+
+        for r in range(ROW_TILES):
+            rows = slice(r * P, (r + 1) * P)
+            logits = bank_pool.tile([P, A], F32, tag="bank", name="logits")
+            nc.tensor.matmul_mx(
+                out=logits[:],
+                lhsT=h2_codes[:, rows].bitcast(FP8X4),
+                lhsT_scale=h2_scale[:, rows],
+                rhs=w3_codes[:].bitcast(FP8X4),
+                rhs_scale=w3_scale[:],
+                start=True,
+                stop=True,
+            )
+            negated = soft.tile([P, A], F32)
+            nc.vector.scalar_tensor_tensor(
+                out=negated[:], in0=logits[:], scalar=-1.0, in1=bias_mask[:, r, :], op0=ALU.mult, op1=ALU.subtract
+            )
+            neg_max = soft.tile([P, 1], F32)
+            nc.vector.tensor_reduce(out=neg_max[:], in_=negated[:], axis=AX.X, op=ALU.min)
+            expd = soft.tile([P, A], F32)
+            row_sum = soft.tile([P, 1], F32)
+            nc.scalar.activation(
+                out=expd[:], in_=negated[:], func=ACT.Exp, bias=neg_max[:], scale=-1.0, accum_out=row_sum[:]
+            )
+            inv_sum = soft.tile([P, 1], F32)
+            nc.vector.reciprocal(out=inv_sum[:], in_=row_sum[:])
+            prob = soft.tile([P, A], F32)
+            nc.vector.tensor_scalar(
+                out=prob[:], in0=expd[:], scalar1=inv_sum[:], scalar2=None, op0=ALU.mult
+            )
+            nc.sync.dma_start(out=out[rows, :], in_=prob[:])

@@ -39,12 +39,21 @@ def tile_dqn_pa_k_kernel(tc, x, h1, W2, b2, W3, b3, out):
         const = ctx.enter_context(tc.tile_pool(name="const", bufs=1))
         h_raw_pool = ctx.enter_context(tc.tile_pool(name="h_raw", bufs=3))
         h_grp_pool = ctx.enter_context(tc.tile_pool(name="h_grp", bufs=2))
-        w_raw_pool = ctx.enter_context(tc.tile_pool(name="w_raw", bufs=6))
-        w_grp_pool = ctx.enter_context(tc.tile_pool(name="w_grp", bufs=4))
-        w_mx_pool = ctx.enter_context(tc.tile_pool(name="w_mx", bufs=4))
+        w_raw_pool = ctx.enter_context(tc.tile_pool(name="w_raw", bufs=8))
+        w_grp_pool = ctx.enter_context(tc.tile_pool(name="w_grp", bufs=6))
+        w_mx_pool = ctx.enter_context(tc.tile_pool(name="w_mx", bufs=6))
         soft = ctx.enter_context(tc.tile_pool(name="soft", bufs=2))
         acc_pool = ctx.enter_context(tc.psum_pool(name="acc", bufs=1))
         bank_pool = ctx.enter_context(tc.psum_pool(name="bank", bufs=4))
+
+        b2_rows = const.tile([H2_TILES, P], BF16)
+        nc.sync.dma_start(out=b2_rows[:], in_=b2.rearrange("(j p) -> j p", p=P))
+        x_sb = const.tile([P, ROW_TILES, A * G], BF16)
+        nc.sync.dma_start(out=x_sb[:], in_=x.rearrange("(r p) c -> p r c", p=P))
+        b3_all = const.tile([P, A], BF16)
+        nc.sync.dma_start(out=b3_all[:], in_=b3.partition_broadcast(P))
+        w3_raw = const.tile([P, PACK, A], BF16)
+        nc.sync.dma_start(out=w3_raw[:], in_=W3.rearrange("(t p) a -> p t a", p=P))
 
         def load_h1(c):
             raw = h_raw_pool.tile([P, ROW_TILES * PERIOD_K], BF16, name="h_raw")
@@ -72,15 +81,6 @@ def tile_dqn_pa_k_kernel(tc, x, h1, W2, b2, W3, b3, out):
                 h_raw[i + H1_LEAD] = load_h1(i + H1_LEAD)
             for c in range(i * W2_LOADS // PERIODS, (i + 1) * W2_LOADS // PERIODS):
                 w_raw[c] = load_w2(c)
-
-        x_sb = const.tile([P, ROW_TILES, A * G], BF16)
-        nc.scalar.dma_start(out=x_sb[:], in_=x.rearrange("(r p) c -> p r c", p=P))
-        w3_raw = const.tile([P, PACK, A], BF16)
-        nc.scalar.dma_start(out=w3_raw[:], in_=W3.rearrange("(t p) a -> p t a", p=P))
-        b3_all = const.tile([P, A], BF16)
-        nc.scalar.dma_start(out=b3_all[:], in_=b3.partition_broadcast(P))
-        b2_rows = const.tile([H2_TILES, P], BF16)
-        nc.scalar.dma_start(out=b2_rows[:], in_=b2.rearrange("(j p) -> j p", p=P))
 
         ident = const.tile([P, P], F32)
         make_identity(nc, ident[:])

@@ -46,15 +46,6 @@ def tile_dqn_pa_k_kernel(tc, x, h1, W2, b2, W3, b3, out):
         acc_pool = ctx.enter_context(tc.psum_pool(name="acc", bufs=1))
         bank_pool = ctx.enter_context(tc.psum_pool(name="bank", bufs=4))
 
-        b2_rows = const.tile([H2_TILES, P], BF16)
-        nc.sync.dma_start(out=b2_rows[:], in_=b2.rearrange("(j p) -> j p", p=P))
-        x_sb = const.tile([P, ROW_TILES, A * G], BF16)
-        nc.sync.dma_start(out=x_sb[:], in_=x.rearrange("(r p) c -> p r c", p=P))
-        b3_all = const.tile([P, A], BF16)
-        nc.sync.dma_start(out=b3_all[:], in_=b3.partition_broadcast(P))
-        w3_raw = const.tile([P, PACK, A], BF16)
-        nc.sync.dma_start(out=w3_raw[:], in_=W3.rearrange("(t p) a -> p t a", p=P))
-
         def load_h1(c):
             raw = h_raw_pool.tile([P, ROW_TILES * PERIOD_K], BF16, name="h_raw")
             nc.sync.dma_start(
@@ -74,13 +65,22 @@ def tile_dqn_pa_k_kernel(tc, x, h1, W2, b2, W3, b3, out):
 
         h_raw = {}
         w_raw = {}
+        b3_square = const.tile([P, A], BF16)
+        nc.vector.memset(b3_square[:], 0.0)
         for c in range(H1_LEAD):
             h_raw[c] = load_h1(c)
+        x_sb = const.tile([P, ROW_TILES, A * G], BF16)
+        nc.sync.dma_start(out=x_sb[:], in_=x.rearrange("(r p) c -> p r c", p=P))
+        b2_rows = const.tile([H2_TILES, P], BF16)
+        nc.sync.dma_start(out=b2_rows[:], in_=b2.rearrange("(j p) -> j p", p=P))
+        nc.sync.dma_start(out=b3_square[0:1, :], in_=b3.unsqueeze(0))
+        w3_raw = const.tile([P, PACK, A], BF16)
+        nc.sync.dma_start(out=w3_raw[:], in_=W3.rearrange("(t p) a -> p t a", p=P))
         for i in range(PERIODS):
+            w_raw[2 * i] = load_w2(2 * i)
             if i + H1_LEAD < PERIODS:
                 h_raw[i + H1_LEAD] = load_h1(i + H1_LEAD)
-            for c in range(i * W2_LOADS // PERIODS, (i + 1) * W2_LOADS // PERIODS):
-                w_raw[c] = load_w2(c)
+            w_raw[2 * i + 1] = load_w2(2 * i + 1)
 
         ident = const.tile([P, P], F32)
         make_identity(nc, ident[:])
@@ -90,36 +90,10 @@ def tile_dqn_pa_k_kernel(tc, x, h1, W2, b2, W3, b3, out):
         one_col = const.tile([P, 1], F32)
         nc.scalar.activation(out=one_col[:], in_=zero_col[:], func=ACT.Exp)
 
+        ones = const.tile([P, P], BF16)
+        nc.vector.memset(ones[:], 1.0)
         b2_square = const.tile([P, P], F32)
         nc.vector.memset(b2_square[:], 0.0)
-        nc.vector.tensor_copy(out=b2_square[0:H2_TILES, :], in_=b2_rows[:])
-        b2_bank = bank_pool.tile([P, P], F32, tag="bank")
-        nc.tensor.transpose(b2_bank[:], b2_square[:], ident[:])
-        b2_col = const.tile([P, H2_TILES], F32)
-        nc.vector.tensor_copy(out=b2_col[:], in_=b2_bank[:, 0:H2_TILES])
-
-        gsum = const.tile([P, ROW_TILES, A], F32)
-        nc.vector.tensor_reduce(
-            out=gsum[:], in_=x_sb[:].rearrange("p r (a g) -> p r a g", g=G), axis=AX.X, op=ALU.add
-        )
-        bias_mask = const.tile([P, ROW_TILES, A], F32)
-        nc.vector.tensor_scalar(
-            out=bias_mask[:], in0=gsum[:], scalar1=0.0, scalar2=MASKED, op0=ALU.is_equal, op1=ALU.mult
-        )
-        for r in range(ROW_TILES):
-            nc.vector.tensor_tensor(
-                out=bias_mask[:, r, :], in0=bias_mask[:, r, :], in1=b3_all[:], op=ALU.add
-            )
-
-        w3_grp = const.tile([P, A, PACK], BF16, align_bytes=64)
-        nc.vector.tensor_copy(out=w3_grp[:], in_=w3_raw[:].rearrange("p t a -> p a t"))
-        w3_codes = const.tile([P, A], U32, align_bytes=64)
-        w3_scale = const.tile([P, A], U8, align_bytes=64)
-        nc.vector.quantize_mx(
-            out=w3_codes[:].bitcast(FP8X4),
-            scales=w3_scale[:],
-            in_=w3_grp[:].rearrange("p a t -> p (a t)"),
-        )
 
         h_codes = const.tile([P, PASSES * B], U32, align_bytes=64)
         h_scale = const.tile([P, PASSES * B], U8, align_bytes=64)
@@ -192,6 +166,37 @@ def tile_dqn_pa_k_kernel(tc, x, h1, W2, b2, W3, b3, out):
             for g in range(PERIOD_PASSES):
                 copy_h1(h_grp, g, banks[g])
             quantise_h1(c, h_grp)
+
+        nc.vector.tensor_copy(out=b2_square[0:H2_TILES, :], in_=b2_rows[:])
+        b2_bank = bank_pool.tile([P, P], F32, tag="bank")
+        nc.tensor.transpose(b2_bank[:], b2_square[:], ident[:])
+        b2_col = const.tile([P, H2_TILES], F32)
+        nc.vector.tensor_copy(out=b2_col[:], in_=b2_bank[:, 0:H2_TILES])
+
+        gsum = const.tile([P, ROW_TILES, A], F32)
+        nc.vector.tensor_reduce(
+            out=gsum[:], in_=x_sb[:].rearrange("p r (a g) -> p r a g", g=G), axis=AX.X, op=ALU.add
+        )
+        bias_mask = const.tile([P, ROW_TILES, A], F32)
+        nc.vector.tensor_scalar(
+            out=bias_mask[:], in0=gsum[:], scalar1=0.0, scalar2=MASKED, op0=ALU.is_equal, op1=ALU.mult
+        )
+        b3_bank = bank_pool.tile([P, A], F32, tag="bank")
+        nc.tensor.matmul(b3_bank[:], lhsT=ones[:], rhs=b3_square[:], start=True, stop=True)
+        for r in range(ROW_TILES):
+            nc.vector.tensor_tensor(
+                out=bias_mask[:, r, :], in0=b3_bank[:], in1=bias_mask[:, r, :], op=ALU.add
+            )
+
+        w3_grp = const.tile([P, A, PACK], BF16, align_bytes=64)
+        nc.vector.tensor_copy(out=w3_grp[:], in_=w3_raw[:].rearrange("p t a -> p a t"))
+        w3_codes = const.tile([P, A], U32, align_bytes=64)
+        w3_scale = const.tile([P, A], U8, align_bytes=64)
+        nc.vector.quantize_mx(
+            out=w3_codes[:].bitcast(FP8X4),
+            scales=w3_scale[:],
+            in_=w3_grp[:].rearrange("p a t -> p (a t)"),
+        )
 
         w_grp = {}
         w_mx = {}

@@ -26,10 +26,10 @@ H2_TILES = H2 // P
 PERIOD_PASSES = 4
 PERIODS = PASSES // PERIOD_PASSES
 PERIOD_K = PERIOD_PASSES * K_PASS
-W2_LOAD_PASSES = 2
-W2_LOADS = PASSES // W2_LOAD_PASSES
 H1_LEAD = 1
-VECTOR_COLS = 288
+H1_AHEAD = 3
+VECTOR_COLS = 272
+VECTOR_COLS_END = 248
 MASKED = -3.0e38
 
 
@@ -42,7 +42,6 @@ def tile_dqn_pa_k_kernel(tc, x, h1, W2, b2, W3, b3, out):
         w_raw_pool = ctx.enter_context(tc.tile_pool(name="w_raw", bufs=8))
         w_grp_pool = ctx.enter_context(tc.tile_pool(name="w_grp", bufs=6))
         w_mx_pool = ctx.enter_context(tc.tile_pool(name="w_mx", bufs=6))
-        soft = ctx.enter_context(tc.tile_pool(name="soft", bufs=2))
         acc_pool = ctx.enter_context(tc.psum_pool(name="acc", bufs=1))
         bank_pool = ctx.enter_context(tc.psum_pool(name="bank", bufs=4))
 
@@ -54,17 +53,19 @@ def tile_dqn_pa_k_kernel(tc, x, h1, W2, b2, W3, b3, out):
             )
             return raw
 
-        def load_w2(c):
-            raw = w_raw_pool.tile([P, W2_LOAD_PASSES, PACK, H2], BF16, name="w_raw")
-            rows = W2[c * W2_LOAD_PASSES * K_PASS : (c + 1) * W2_LOAD_PASSES * K_PASS, :]
+        w_raw = {}
+
+        def load_w2(first, n):
+            raw = w_raw_pool.tile([P, n, PACK, H2], BF16, name="w_raw")
+            rows = W2[first * K_PASS : (first + n) * K_PASS, :]
             nc.sync.dma_start(
                 out=raw[:].rearrange("p g (u e) n -> p (g u) (e n)", u=2),
-                in_=rows.rearrange("(g u p e) n -> p (g u) (e n)", g=W2_LOAD_PASSES, u=2, p=P),
+                in_=rows.rearrange("(g u p e) n -> p (g u) (e n)", g=n, u=2, p=P),
             )
-            return raw
+            for s in range(n):
+                w_raw[first + s] = raw[:, s]
 
         h_raw = {}
-        w_raw = {}
         b3_square = const.tile([P, A], BF16)
         nc.vector.memset(b3_square[:], 0.0)
         for c in range(H1_LEAD):
@@ -77,10 +78,13 @@ def tile_dqn_pa_k_kernel(tc, x, h1, W2, b2, W3, b3, out):
         w3_raw = const.tile([P, PACK, A], BF16)
         nc.sync.dma_start(out=w3_raw[:], in_=W3.rearrange("(t p) a -> p t a", p=P))
         for i in range(PERIODS):
-            w_raw[2 * i] = load_w2(2 * i)
+            load_w2(4 * i, 2)
             if i + H1_LEAD < PERIODS:
                 h_raw[i + H1_LEAD] = load_h1(i + H1_LEAD)
-            w_raw[2 * i + 1] = load_w2(2 * i + 1)
+            if i + 1 < PERIODS:
+                load_w2(4 * i + 2, 2)
+        load_w2(PASSES - 2, 1)
+        load_w2(PASSES - 1, 1)
 
         ident = const.tile([P, P], F32)
         make_identity(nc, ident[:])
@@ -99,51 +103,59 @@ def tile_dqn_pa_k_kernel(tc, x, h1, W2, b2, W3, b3, out):
         h_scale = const.tile([P, PASSES * B], U8, align_bytes=64)
         acc = [acc_pool.tile([P, B], F32, name="acc%d" % j) for j in range(H2_TILES)]
 
-        def transpose_h1(c):
-            words = h_raw[c][:].bitcast(F32)
-            banks = []
-            for g in range(PERIOD_PASSES):
-                bank = bank_pool.tile([P, 2, B], F32, tag="bank", name="h_bank")
-                for u in range(2):
-                    for r in range(ROW_TILES):
-                        first = r * PERIOD_K // 2 + (2 * g + u) * P
-                        nc.tensor.transpose(
-                            bank[:, u, r * P : (r + 1) * P], words[:, first : first + P], ident[:]
-                        )
-                banks.append(bank)
-            return banks
+        def transpose_h1(g):
+            words = h_raw[g // PERIOD_PASSES][:].bitcast(F32)
+            bank = bank_pool.tile([P, 2, B], F32, tag="bank", name="h_bank")
+            for u in range(2):
+                for r in range(ROW_TILES):
+                    first = r * PERIOD_K // 2 + (2 * (g % PERIOD_PASSES) + u) * P
+                    nc.tensor.transpose(
+                        bank[:, u, r * P : (r + 1) * P], words[:, first : first + P], ident[:]
+                    )
+            return bank
 
-        def copy_h1(grp, g, bank):
-            pairs = grp[:].bitcast(F32)[:, g * 2 * B : (g + 1) * 2 * B]
+        h_grp = {}
+
+        def copy_h1(g, bank):
+            c, s = g // PERIOD_PASSES, g % PERIOD_PASSES
+            if s == 0:
+                h_grp[c] = h_grp_pool.tile(
+                    [P, PERIOD_PASSES * B * PACK], BF16, align_bytes=64, name="h_grp"
+                )
+            pairs = h_grp[c][:].bitcast(F32)[:, s * 2 * B : (s + 1) * 2 * B]
             nc.scalar.copy(
                 out=pairs.rearrange("p (i u) -> p i u", u=2), in_=bank[:].rearrange("p u i -> p i u")
             )
 
-        def quantise_h1(c, grp):
+        def quantise_h1(c):
             cols = slice(c * PERIOD_PASSES * B, (c + 1) * PERIOD_PASSES * B)
             nc.vector.quantize_mx(
-                out=h_codes[:, cols].bitcast(FP8X4), scales=h_scale[:, cols], in_=grp[:]
+                out=h_codes[:, cols].bitcast(FP8X4), scales=h_scale[:, cols], in_=h_grp[c][:]
             )
 
         def regroup_w2(g):
-            rows = w_raw[g // W2_LOAD_PASSES][:, g % W2_LOAD_PASSES]
+            rows = w_raw[g]
+            cut = VECTOR_COLS if g + H1_AHEAD < PASSES else VECTOR_COLS_END
             grp = w_grp_pool.tile([P, H2, PACK], BF16, align_bytes=64, name="w_grp")
             nc.vector.tensor_copy(
-                out=grp[:, 0:VECTOR_COLS, :].rearrange("p (c i) t -> p c t i", i=4),
-                in_=rows[:, :, 0:VECTOR_COLS].rearrange("p t (c i) -> p c t i", i=4),
+                out=grp[:, 0:cut, :].rearrange("p (c i) t -> p c t i", i=4),
+                in_=rows[:, :, 0:cut].rearrange("p t (c i) -> p c t i", i=4),
             )
             nc.scalar.copy(
-                out=grp[:, VECTOR_COLS:H2, :].rearrange("p (c i) t -> p c t i", i=4),
-                in_=rows[:, :, VECTOR_COLS:H2].rearrange("p t (c i) -> p c t i", i=4),
+                out=grp[:, cut:H2, :].rearrange("p (c i) t -> p c t i", i=4),
+                in_=rows[:, :, cut:H2].rearrange("p t (c i) -> p c t i", i=4),
             )
             return grp
 
-        def quantise_w2(grp):
+        def quantise_w2(grp, halves):
             codes = w_mx_pool.tile([P, H2], U32, align_bytes=64, name="w_codes")
             scale = w_mx_pool.tile([P, H2], U8, align_bytes=64, name="w_scale")
-            nc.vector.quantize_mx(
-                out=codes[:].bitcast(FP8X4), scales=scale[:], in_=grp[:].rearrange("p n t -> p (n t)")
-            )
+            for cols in halves:
+                nc.vector.quantize_mx(
+                    out=codes[:, cols].bitcast(FP8X4),
+                    scales=scale[:, cols],
+                    in_=grp[:, cols, :].rearrange("p n t -> p (n t)"),
+                )
             return codes, scale
 
         def multiply(g, codes, scale):
@@ -160,12 +172,13 @@ def tile_dqn_pa_k_kernel(tc, x, h1, W2, b2, W3, b3, out):
                     stop=(g == PASSES - 1),
                 )
 
-        for c in range(H1_LEAD):
-            banks = transpose_h1(c)
-            h_grp = h_grp_pool.tile([P, PERIOD_PASSES * B * PACK], BF16, align_bytes=64, name="h_grp")
+        banks = {}
+        with tc.manual_schedule():
             for g in range(PERIOD_PASSES):
-                copy_h1(h_grp, g, banks[g])
-            quantise_h1(c, h_grp)
+                banks[g] = transpose_h1(g)
+            for g in range(PERIOD_PASSES):
+                copy_h1(g, banks[g])
+            quantise_h1(0)
 
         nc.vector.tensor_copy(out=b2_square[0:H2_TILES, :], in_=b2_rows[:])
         b2_bank = bank_pool.tile([P, P], F32, tag="bank")
@@ -200,27 +213,25 @@ def tile_dqn_pa_k_kernel(tc, x, h1, W2, b2, W3, b3, out):
 
         w_grp = {}
         w_mx = {}
-        for i in range(PERIODS):
-            c = i + H1_LEAD
-            if c < PERIODS:
-                banks = transpose_h1(c)
-                h_grp = h_grp_pool.tile(
-                    [P, PERIOD_PASSES * B * PACK], BF16, align_bytes=64, name="h_grp"
-                )
-            for s in range(PERIOD_PASSES):
-                g = i * PERIOD_PASSES + s
-                if c < PERIODS:
-                    copy_h1(h_grp, s, banks[s])
-                w_grp[g] = regroup_w2(g)
-                if g >= 1:
-                    w_mx[g - 1] = quantise_w2(w_grp[g - 1])
+        with tc.manual_schedule():
+            for g in range(PASSES + 2):
+                h = g + H1_AHEAD
+                if h + 1 < PASSES:
+                    banks[h + 1] = transpose_h1(h + 1)
+                if g < PASSES:
+                    w_grp[g] = regroup_w2(g)
+                if PERIOD_PASSES <= h < PASSES:
+                    copy_h1(h, banks[h])
+                if 1 <= g <= PASSES:
+                    parts = 2 if g == PASSES else 1
+                    width = H2 // parts
+                    w_mx[g - 1] = quantise_w2(
+                        w_grp[g - 1], [slice(i * width, (i + 1) * width) for i in range(parts)]
+                    )
+                if PERIOD_PASSES < h <= PASSES and h % PERIOD_PASSES == 0:
+                    quantise_h1(h // PERIOD_PASSES - 1)
                 if g >= 2:
                     multiply(g - 2, w_mx[g - 2][0], w_mx[g - 2][1])
-            if c < PERIODS:
-                quantise_h1(c, h_grp)
-        w_mx[PASSES - 1] = quantise_w2(w_grp[PASSES - 1])
-        multiply(PASSES - 2, w_mx[PASSES - 2][0], w_mx[PASSES - 2][1])
-        multiply(PASSES - 1, w_mx[PASSES - 1][0], w_mx[PASSES - 1][1])
 
         pre = const.tile([P, H2_TILES, B], F32)
         for j in range(H2_TILES):
@@ -249,11 +260,11 @@ def tile_dqn_pa_k_kernel(tc, x, h1, W2, b2, W3, b3, out):
                 in_=h2_grp[:, rows, :].rearrange("p i t -> p (i t)"),
             )
 
+        logits = bank_pool.tile([P, ROW_TILES, A], F32, tag="bank", name="logits")
         for r in range(ROW_TILES):
             rows = slice(r * P, (r + 1) * P)
-            logits = bank_pool.tile([P, A], F32, tag="bank", name="logits")
             nc.tensor.matmul_mx(
-                out=logits[:],
+                out=logits[:, r, :],
                 lhsT=h2_codes[:, rows].bitcast(FP8X4),
                 lhsT_scale=h2_scale[:, rows],
                 rhs=w3_codes[:].bitcast(FP8X4),
@@ -261,21 +272,28 @@ def tile_dqn_pa_k_kernel(tc, x, h1, W2, b2, W3, b3, out):
                 start=True,
                 stop=True,
             )
-            negated = soft.tile([P, A], F32)
-            nc.vector.scalar_tensor_tensor(
-                out=negated[:], in0=logits[:], scalar=-1.0, in1=bias_mask[:, r, :], op0=ALU.mult, op1=ALU.subtract
-            )
-            neg_max = soft.tile([P, 1], F32)
-            nc.vector.tensor_reduce(out=neg_max[:], in_=negated[:], axis=AX.X, op=ALU.min)
-            expd = soft.tile([P, A], F32)
-            row_sum = soft.tile([P, 1], F32)
+        negated = const.tile([P, ROW_TILES, A], F32)
+        nc.vector.scalar_tensor_tensor(
+            out=negated[:], in0=logits[:], scalar=-1.0, in1=bias_mask[:], op0=ALU.mult, op1=ALU.subtract
+        )
+        neg_max = const.tile([P, ROW_TILES], F32)
+        nc.vector.tensor_reduce(out=neg_max[:], in_=negated[:], axis=AX.X, op=ALU.min)
+        expd = const.tile([P, ROW_TILES, A], F32)
+        row_sum = const.tile([P, ROW_TILES], F32)
+        for r in range(ROW_TILES):
             nc.scalar.activation(
-                out=expd[:], in_=negated[:], func=ACT.Exp, bias=neg_max[:], scale=-1.0, accum_out=row_sum[:]
+                out=expd[:, r, :],
+                in_=negated[:, r, :],
+                func=ACT.Exp,
+                bias=neg_max[:, r : r + 1],
+                scale=-1.0,
+                accum_out=row_sum[:, r : r + 1],
             )
-            inv_sum = soft.tile([P, 1], F32)
-            nc.vector.reciprocal(out=inv_sum[:], in_=row_sum[:])
-            prob = soft.tile([P, A], F32)
+        inv_sum = const.tile([P, ROW_TILES], F32)
+        prob = const.tile([P, ROW_TILES, A], F32)
+        for r in range(ROW_TILES):
+            nc.vector.reciprocal(out=inv_sum[:, r : r + 1], in_=row_sum[:, r : r + 1])
             nc.vector.tensor_scalar(
-                out=prob[:], in0=expd[:], scalar1=inv_sum[:], scalar2=None, op0=ALU.mult
+                out=prob[:, r, :], in0=expd[:, r, :], scalar1=inv_sum[:, r : r + 1], scalar2=None, op0=ALU.mult
             )
-            nc.sync.dma_start(out=out[rows, :], in_=prob[:])
+        nc.sync.dma_start(out=out.rearrange("(r p) a -> p r a", p=P), in_=prob[:])

@@ -24,9 +24,6 @@ ROW_TILES = B // P
 H2_TILES = H2 // P
 
 PERIOD_PASSES = 4
-PERIODS = PASSES // PERIOD_PASSES
-PERIOD_K = PERIOD_PASSES * K_PASS
-H1_LEAD = 1
 H1_AHEAD = 3
 VECTOR_COLS = 272
 VECTOR_COLS_END = 248
@@ -45,13 +42,16 @@ def tile_dqn_pa_k_kernel(tc, x, h1, W2, b2, W3, b3, out):
         acc_pool = ctx.enter_context(tc.psum_pool(name="acc", bufs=1))
         bank_pool = ctx.enter_context(tc.psum_pool(name="bank", bufs=4))
 
-        def load_h1(c):
-            raw = h_raw_pool.tile([P, ROW_TILES * PERIOD_K], BF16, name="h_raw")
+        h_raw = {}
+
+        def load_h1(first, n):
+            raw = h_raw_pool.tile([P, ROW_TILES, n * K_PASS], BF16, name="h_raw")
             nc.sync.dma_start(
-                out=raw[:].rearrange("p (r k) -> p r k", r=ROW_TILES),
-                in_=h1[:, c * PERIOD_K : (c + 1) * PERIOD_K].rearrange("(r p) k -> p r k", p=P),
+                out=raw[:],
+                in_=h1[:, first * K_PASS : (first + n) * K_PASS].rearrange("(p r) k -> p r k", p=P),
             )
-            return raw
+            for s in range(n):
+                h_raw[first + s] = raw[:, :, s * K_PASS : (s + 1) * K_PASS]
 
         w_raw = {}
 
@@ -59,30 +59,27 @@ def tile_dqn_pa_k_kernel(tc, x, h1, W2, b2, W3, b3, out):
             raw = w_raw_pool.tile([P, n, PACK, H2], BF16, name="w_raw")
             rows = W2[first * K_PASS : (first + n) * K_PASS, :]
             nc.sync.dma_start(
-                out=raw[:].rearrange("p g (u e) n -> p (g u) (e n)", u=2),
-                in_=rows.rearrange("(g u p e) n -> p (g u) (e n)", g=n, u=2, p=P),
+                out=raw[:].rearrange("p g t n -> p g (t n)"),
+                in_=rows.rearrange("(g p t) n -> p g (t n)", g=n, p=P),
             )
             for s in range(n):
                 w_raw[first + s] = raw[:, s]
 
-        h_raw = {}
         b3_square = const.tile([P, A], BF16)
         nc.vector.memset(b3_square[:], 0.0)
-        for c in range(H1_LEAD):
-            h_raw[c] = load_h1(c)
+        load_h1(0, 4)
         x_sb = const.tile([P, ROW_TILES, A * G], BF16)
-        nc.sync.dma_start(out=x_sb[:], in_=x.rearrange("(r p) c -> p r c", p=P))
+        nc.sync.dma_start(out=x_sb[:], in_=x.rearrange("(p r) c -> p r c", p=P))
         b2_rows = const.tile([H2_TILES, P], BF16)
         nc.sync.dma_start(out=b2_rows[:], in_=b2.rearrange("(j p) -> j p", p=P))
         nc.sync.dma_start(out=b3_square[0:1, :], in_=b3.unsqueeze(0))
         w3_raw = const.tile([P, PACK, A], BF16)
         nc.sync.dma_start(out=w3_raw[:], in_=W3.rearrange("(t p) a -> p t a", p=P))
-        for i in range(PERIODS):
-            load_w2(4 * i, 2)
-            if i + H1_LEAD < PERIODS:
-                h_raw[i + H1_LEAD] = load_h1(i + H1_LEAD)
-            if i + 1 < PERIODS:
-                load_w2(4 * i + 2, 2)
+        h1_loads = {2: (4, 4), 6: (8, 8), 12: (16, 8), 20: (24, 8)}
+        for g in range(0, PASSES - 2, 2):
+            if g in h1_loads:
+                load_h1(*h1_loads[g])
+            load_w2(g, 2)
         load_w2(PASSES - 2, 1)
         load_w2(PASSES - 1, 1)
 
@@ -104,14 +101,11 @@ def tile_dqn_pa_k_kernel(tc, x, h1, W2, b2, W3, b3, out):
         acc = [acc_pool.tile([P, B], F32, name="acc%d" % j) for j in range(H2_TILES)]
 
         def transpose_h1(g):
-            words = h_raw[g // PERIOD_PASSES][:].bitcast(F32)
             bank = bank_pool.tile([P, 2, B], F32, tag="bank", name="h_bank")
             for u in range(2):
                 for r in range(ROW_TILES):
-                    first = r * PERIOD_K // 2 + (2 * (g % PERIOD_PASSES) + u) * P
-                    nc.tensor.transpose(
-                        bank[:, u, r * P : (r + 1) * P], words[:, first : first + P], ident[:]
-                    )
+                    words = h_raw[g][:, r, :].bitcast(F32)
+                    nc.tensor.transpose(bank[:, u, r * P : (r + 1) * P], words[:, u::2], ident[:])
             return bank
 
         h_grp = {}
@@ -296,4 +290,4 @@ def tile_dqn_pa_k_kernel(tc, x, h1, W2, b2, W3, b3, out):
             nc.vector.tensor_scalar(
                 out=prob[:, r, :], in0=expd[:, r, :], scalar1=inv_sum[:, r : r + 1], scalar2=None, op0=ALU.mult
             )
-        nc.sync.dma_start(out=out.rearrange("(r p) a -> p r a", p=P), in_=prob[:])
+        nc.sync.dma_start(out=out.rearrange("(p r) a -> p r a", p=P), in_=prob[:])

@@ -67,7 +67,7 @@ def tile_dqn_pa_k_kernel(tc, x, h1, W2, b2, W3, b3, out):
 
         b3_square = const.tile([P, A], BF16)
         nc.vector.memset(b3_square[:], 0.0)
-        load_h1(0, 4)
+        load_h1(0, PERIOD_PASSES)
         x_sb = const.tile([P, ROW_TILES, A * G], BF16)
         nc.sync.dma_start(out=x_sb[:], in_=x.rearrange("(p r) c -> p r c", p=P))
         b2_rows = const.tile([H2_TILES, P], BF16)
@@ -75,10 +75,9 @@ def tile_dqn_pa_k_kernel(tc, x, h1, W2, b2, W3, b3, out):
         nc.sync.dma_start(out=b3_square[0:1, :], in_=b3.unsqueeze(0))
         w3_raw = const.tile([P, PACK, A], BF16)
         nc.sync.dma_start(out=w3_raw[:], in_=W3.rearrange("(t p) a -> p t a", p=P))
-        h1_loads = {2: (4, 4), 6: (8, 8), 12: (16, 8), 20: (24, 8)}
         for g in range(0, PASSES - 2, 2):
-            if g in h1_loads:
-                load_h1(*h1_loads[g])
+            if (g + 2) % PERIOD_PASSES == 0:
+                load_h1(g + 2, PERIOD_PASSES)
             load_w2(g, 2)
         load_w2(PASSES - 2, 1)
         load_w2(PASSES - 1, 1)

@@ -24,7 +24,7 @@ ROW_TILES = B // P
 H2_TILES = H2 // P
 
 PERIOD_PASSES = 4
-H1_AHEAD = 3
+H1_AHEAD = 2
 VECTOR_COLS = 272
 VECTOR_COLS_END = 248
 MASKED = -3.0e38
@@ -36,9 +36,10 @@ def tile_dqn_pa_k_kernel(tc, x, h1, W2, b2, W3, b3, out):
         const = ctx.enter_context(tc.tile_pool(name="const", bufs=1))
         h_raw_pool = ctx.enter_context(tc.tile_pool(name="h_raw", bufs=3))
         h_grp_pool = ctx.enter_context(tc.tile_pool(name="h_grp", bufs=2))
-        w_raw_pool = ctx.enter_context(tc.tile_pool(name="w_raw", bufs=8))
+        w_raw_pool = ctx.enter_context(tc.tile_pool(name="w_raw", bufs=16))
         w_grp_pool = ctx.enter_context(tc.tile_pool(name="w_grp", bufs=6))
         w_mx_pool = ctx.enter_context(tc.tile_pool(name="w_mx", bufs=6))
+        soft = ctx.enter_context(tc.tile_pool(name="soft", bufs=2))
         acc_pool = ctx.enter_context(tc.psum_pool(name="acc", bufs=1))
         bank_pool = ctx.enter_context(tc.psum_pool(name="bank", bufs=4))
 
@@ -55,15 +56,12 @@ def tile_dqn_pa_k_kernel(tc, x, h1, W2, b2, W3, b3, out):
 
         w_raw = {}
 
-        def load_w2(first, n):
-            raw = w_raw_pool.tile([P, n, PACK, H2], BF16, name="w_raw")
-            rows = W2[first * K_PASS : (first + n) * K_PASS, :]
+        def load_w2(g):
+            w_raw[g] = w_raw_pool.tile([P, PACK, H2], BF16, name="w_raw")
             nc.sync.dma_start(
-                out=raw[:].rearrange("p g t n -> p g (t n)"),
-                in_=rows.rearrange("(g p t) n -> p g (t n)", g=n, p=P),
+                out=w_raw[g][:],
+                in_=W2[g * K_PASS : (g + 1) * K_PASS, :].rearrange("(p t) n -> p t n", p=P),
             )
-            for s in range(n):
-                w_raw[first + s] = raw[:, s]
 
         b3_square = const.tile([P, A], BF16)
         nc.vector.memset(b3_square[:], 0.0)
@@ -75,12 +73,10 @@ def tile_dqn_pa_k_kernel(tc, x, h1, W2, b2, W3, b3, out):
         nc.sync.dma_start(out=b3_square[0:1, :], in_=b3.unsqueeze(0))
         w3_raw = const.tile([P, PACK, A], BF16)
         nc.sync.dma_start(out=w3_raw[:], in_=W3.rearrange("(t p) a -> p t a", p=P))
-        for g in range(0, PASSES - 2, 2):
-            if (g + 2) % PERIOD_PASSES == 0:
+        for g in range(PASSES):
+            if (g + 2) % PERIOD_PASSES == 0 and g + 2 < PASSES:
                 load_h1(g + 2, PERIOD_PASSES)
-            load_w2(g, 2)
-        load_w2(PASSES - 2, 1)
-        load_w2(PASSES - 1, 1)
+            load_w2(g)
 
         ident = const.tile([P, P], F32)
         make_identity(nc, ident[:])
@@ -209,20 +205,20 @@ def tile_dqn_pa_k_kernel(tc, x, h1, W2, b2, W3, b3, out):
         with tc.manual_schedule():
             for g in range(PASSES + 2):
                 h = g + H1_AHEAD
-                if h + 1 < PASSES:
+                if PERIOD_PASSES <= h + 1 < PASSES:
                     banks[h + 1] = transpose_h1(h + 1)
-                if g < PASSES:
-                    w_grp[g] = regroup_w2(g)
                 if PERIOD_PASSES <= h < PASSES:
                     copy_h1(h, banks[h])
+                if g < PASSES:
+                    w_grp[g] = regroup_w2(g)
                 if 1 <= g <= PASSES:
                     parts = 2 if g == PASSES else 1
                     width = H2 // parts
                     w_mx[g - 1] = quantise_w2(
                         w_grp[g - 1], [slice(i * width, (i + 1) * width) for i in range(parts)]
                     )
-                if PERIOD_PASSES < h <= PASSES and h % PERIOD_PASSES == 0:
-                    quantise_h1(h // PERIOD_PASSES - 1)
+                if PERIOD_PASSES <= h < PASSES and (h + 1) % PERIOD_PASSES == 0:
+                    quantise_h1(h // PERIOD_PASSES)
                 if g >= 2:
                     multiply(g - 2, w_mx[g - 2][0], w_mx[g - 2][1])
 
@@ -253,11 +249,12 @@ def tile_dqn_pa_k_kernel(tc, x, h1, W2, b2, W3, b3, out):
                 in_=h2_grp[:, rows, :].rearrange("p i t -> p (i t)"),
             )
 
-        logits = bank_pool.tile([P, ROW_TILES, A], F32, tag="bank", name="logits")
+        logits, negated, neg_max, expd, row_sum = {}, {}, {}, {}, {}
         for r in range(ROW_TILES):
             rows = slice(r * P, (r + 1) * P)
+            logits[r] = bank_pool.tile([P, A], F32, tag="bank", name="logits")
             nc.tensor.matmul_mx(
-                out=logits[:, r, :],
+                out=logits[r][:],
                 lhsT=h2_codes[:, rows].bitcast(FP8X4),
                 lhsT_scale=h2_scale[:, rows],
                 rhs=w3_codes[:].bitcast(FP8X4),
@@ -265,28 +262,36 @@ def tile_dqn_pa_k_kernel(tc, x, h1, W2, b2, W3, b3, out):
                 start=True,
                 stop=True,
             )
-        negated = const.tile([P, ROW_TILES, A], F32)
-        nc.vector.scalar_tensor_tensor(
-            out=negated[:], in0=logits[:], scalar=-1.0, in1=bias_mask[:], op0=ALU.mult, op1=ALU.subtract
-        )
-        neg_max = const.tile([P, ROW_TILES], F32)
-        nc.vector.tensor_reduce(out=neg_max[:], in_=negated[:], axis=AX.X, op=ALU.min)
-        expd = const.tile([P, ROW_TILES, A], F32)
-        row_sum = const.tile([P, ROW_TILES], F32)
-        for r in range(ROW_TILES):
-            nc.scalar.activation(
-                out=expd[:, r, :],
-                in_=negated[:, r, :],
-                func=ACT.Exp,
-                bias=neg_max[:, r : r + 1],
-                scale=-1.0,
-                accum_out=row_sum[:, r : r + 1],
-            )
-        inv_sum = const.tile([P, ROW_TILES], F32)
-        prob = const.tile([P, ROW_TILES, A], F32)
-        for r in range(ROW_TILES):
-            nc.vector.reciprocal(out=inv_sum[:, r : r + 1], in_=row_sum[:, r : r + 1])
-            nc.vector.tensor_scalar(
-                out=prob[:, r, :], in0=expd[:, r, :], scalar1=inv_sum[:, r : r + 1], scalar2=None, op0=ALU.mult
-            )
-        nc.sync.dma_start(out=out.rearrange("(p r) a -> p r a", p=P), in_=prob[:])
+        with tc.manual_schedule():
+            for r in range(ROW_TILES):
+                negated[r] = soft.tile([P, A], F32, name="negated")
+                nc.vector.scalar_tensor_tensor(
+                    out=negated[r][:],
+                    in0=logits[r][:],
+                    scalar=-1.0,
+                    in1=bias_mask[:, r, :],
+                    op0=ALU.mult,
+                    op1=ALU.subtract,
+                )
+            for r in range(ROW_TILES):
+                neg_max[r] = soft.tile([P, 1], F32, name="neg_max")
+                nc.vector.tensor_reduce(out=neg_max[r][:], in_=negated[r][:], axis=AX.X, op=ALU.min)
+            for r in range(ROW_TILES):
+                expd[r] = soft.tile([P, A], F32, name="expd")
+                row_sum[r] = soft.tile([P, 1], F32, name="row_sum")
+                nc.scalar.activation(
+                    out=expd[r][:],
+                    in_=negated[r][:],
+                    func=ACT.Exp,
+                    bias=neg_max[r][:],
+                    scale=-1.0,
+                    accum_out=row_sum[r][:],
+                )
+            for r in range(ROW_TILES):
+                inv_sum = soft.tile([P, 1], F32, name="inv_sum")
+                nc.vector.reciprocal(out=inv_sum[:], in_=row_sum[r][:])
+                prob = soft.tile([P, A], F32, name="prob")
+                nc.vector.tensor_scalar(
+                    out=prob[:], in0=expd[r][:], scalar1=inv_sum[:], scalar2=None, op0=ALU.mult
+                )
+                nc.sync.dma_start(out=out.rearrange("(p r) a -> r p a", p=P)[r], in_=prob[:])

@@ -26,7 +26,8 @@ H2_TILES = H2 // P
 PERIOD_PASSES = 4
 H1_AHEAD = 2
 VECTOR_COLS = 272
-VECTOR_COLS_END = 248
+VECTOR_COLS_END = 240
+RUN = 8
 MASKED = -3.0e38
 
 
@@ -127,12 +128,12 @@ def tile_dqn_pa_k_kernel(tc, x, h1, W2, b2, W3, b3, out):
             cut = VECTOR_COLS if g + H1_AHEAD < PASSES else VECTOR_COLS_END
             grp = w_grp_pool.tile([P, H2, PACK], BF16, align_bytes=64, name="w_grp")
             nc.vector.tensor_copy(
-                out=grp[:, 0:cut, :].rearrange("p (c i) t -> p c t i", i=4),
-                in_=rows[:, :, 0:cut].rearrange("p t (c i) -> p c t i", i=4),
+                out=grp[:, 0:cut, :].rearrange("p (c i) t -> p c t i", i=RUN),
+                in_=rows[:, :, 0:cut].rearrange("p t (c i) -> p c t i", i=RUN),
             )
             nc.scalar.copy(
-                out=grp[:, cut:H2, :].rearrange("p (c i) t -> p c t i", i=4),
-                in_=rows[:, :, cut:H2].rearrange("p t (c i) -> p c t i", i=4),
+                out=grp[:, cut:H2, :].rearrange("p (c i) t -> p c t i", i=RUN),
+                in_=rows[:, :, cut:H2].rearrange("p t (c i) -> p c t i", i=RUN),
             )
             return grp
 

@@ -24,9 +24,10 @@ ROW_TILES = B // P
 H2_TILES = H2 // P
 
 PERIOD_PASSES = 4
+GROUP_PASSES = 2
 H1_AHEAD = 2
-VECTOR_COLS = 272
-VECTOR_COLS_END = 240
+VECTOR_COLS = 288
+VECTOR_COLS_END = 256
 RUN = 8
 MASKED = -3.0e38
 
@@ -36,7 +37,7 @@ def tile_dqn_pa_k_kernel(tc, x, h1, W2, b2, W3, b3, out):
     with ExitStack() as ctx:
         const = ctx.enter_context(tc.tile_pool(name="const", bufs=1))
         h_raw_pool = ctx.enter_context(tc.tile_pool(name="h_raw", bufs=3))
-        h_grp_pool = ctx.enter_context(tc.tile_pool(name="h_grp", bufs=2))
+        h_grp_pool = ctx.enter_context(tc.tile_pool(name="h_grp", bufs=4))
         w_raw_pool = ctx.enter_context(tc.tile_pool(name="w_raw", bufs=16))
         w_grp_pool = ctx.enter_context(tc.tile_pool(name="w_grp", bufs=6))
         w_mx_pool = ctx.enter_context(tc.tile_pool(name="w_mx", bufs=6))
@@ -107,10 +108,10 @@ def tile_dqn_pa_k_kernel(tc, x, h1, W2, b2, W3, b3, out):
         h_grp = {}
 
         def copy_h1(g, bank):
-            c, s = g // PERIOD_PASSES, g % PERIOD_PASSES
+            c, s = g // GROUP_PASSES, g % GROUP_PASSES
             if s == 0:
                 h_grp[c] = h_grp_pool.tile(
-                    [P, PERIOD_PASSES * B * PACK], BF16, align_bytes=64, name="h_grp"
+                    [P, GROUP_PASSES * B * PACK], BF16, align_bytes=64, name="h_grp"
                 )
             pairs = h_grp[c][:].bitcast(F32)[:, s * 2 * B : (s + 1) * 2 * B]
             nc.scalar.copy(
@@ -118,7 +119,7 @@ def tile_dqn_pa_k_kernel(tc, x, h1, W2, b2, W3, b3, out):
             )
 
         def quantise_h1(c):
-            cols = slice(c * PERIOD_PASSES * B, (c + 1) * PERIOD_PASSES * B)
+            cols = slice(c * GROUP_PASSES * B, (c + 1) * GROUP_PASSES * B)
             nc.vector.quantize_mx(
                 out=h_codes[:, cols].bitcast(FP8X4), scales=h_scale[:, cols], in_=h_grp[c][:]
             )
@@ -168,7 +169,8 @@ def tile_dqn_pa_k_kernel(tc, x, h1, W2, b2, W3, b3, out):
                 banks[g] = transpose_h1(g)
             for g in range(PERIOD_PASSES):
                 copy_h1(g, banks[g])
-            quantise_h1(0)
+            for c in range(PERIOD_PASSES // GROUP_PASSES):
+                quantise_h1(c)
 
         nc.vector.tensor_copy(out=b2_square[0:H2_TILES, :], in_=b2_rows[:])
         b2_bank = bank_pool.tile([P, P], F32, tag="bank")
@@ -218,8 +220,8 @@ def tile_dqn_pa_k_kernel(tc, x, h1, W2, b2, W3, b3, out):
                     w_mx[g - 1] = quantise_w2(
                         w_grp[g - 1], [slice(i * width, (i + 1) * width) for i in range(parts)]
                     )
-                if PERIOD_PASSES <= h < PASSES and (h + 1) % PERIOD_PASSES == 0:
-                    quantise_h1(h // PERIOD_PASSES)
+                if PERIOD_PASSES <= h < PASSES and (h + 1) % GROUP_PASSES == 0:
+                    quantise_h1(h // GROUP_PASSES)
                 if g >= 2:
                     multiply(g - 2, w_mx[g - 2][0], w_mx[g - 2][1])
 
@@ -250,7 +252,7 @@ def tile_dqn_pa_k_kernel(tc, x, h1, W2, b2, W3, b3, out):
                 in_=h2_grp[:, rows, :].rearrange("p i t -> p (i t)"),
             )
 
-        logits, negated, neg_max, expd, row_sum = {}, {}, {}, {}, {}
+        logits, negated, neg_max, expd, row_sum, inv_sum = {}, {}, {}, {}, {}, {}
         for r in range(ROW_TILES):
             rows = slice(r * P, (r + 1) * P)
             logits[r] = bank_pool.tile([P, A], F32, tag="bank", name="logits")
@@ -289,10 +291,11 @@ def tile_dqn_pa_k_kernel(tc, x, h1, W2, b2, W3, b3, out):
                     accum_out=row_sum[r][:],
                 )
             for r in range(ROW_TILES):
-                inv_sum = soft.tile([P, 1], F32, name="inv_sum")
-                nc.vector.reciprocal(out=inv_sum[:], in_=row_sum[r][:])
+                inv_sum[r] = soft.tile([P, 1], F32, name="inv_sum")
+                nc.vector.reciprocal(out=inv_sum[r][:], in_=row_sum[r][:])
+            for r in range(ROW_TILES):
                 prob = soft.tile([P, A], F32, name="prob")
                 nc.vector.tensor_scalar(
-                    out=prob[:], in0=expd[r][:], scalar1=inv_sum[:], scalar2=None, op0=ALU.mult
+                    out=prob[:], in0=expd[r][:], scalar1=inv_sum[r][:], scalar2=None, op0=ALU.mult
                 )
                 nc.sync.dma_start(out=out.rearrange("(p r) a -> r p a", p=P)[r], in_=prob[:])

from contextlib import ExitStack

import concourse.mybir as mybir
from concourse.masks import make_identity

F32 = mybir.dt.float32
BF16 = mybir.dt.bfloat16
U32 = mybir.dt.uint32
U8 = mybir.dt.uint8
FP8X4 = mybir.dt.float8_e4m3fn_x4
ALU = mybir.AluOpType
ACT = mybir.ActivationFunctionType
AX = mybir.AxisListType

B, A, G, H1, H2 = 256, 128, 5, 16384, 512
SLOPE = 0.4
FLOPS = 2 * B * H1 * H2 + 2 * B * H2 * A

P = 128
PACK = 4
K_PASS = P * PACK
PASSES = H1 // K_PASS
ROW_TILES = B // P
H2_TILES = H2 // P

PERIOD_PASSES = 4
GROUP_PASSES = 2
H1_AHEAD = 2
VECTOR_COLS = 288
VECTOR_COLS_END = 256
RUN = 8
MASKED = -3.0e38


def tile_dqn_pa_k_kernel(tc, x, h1, W2, b2, W3, b3, out):
    nc = tc.nc
    with ExitStack() as ctx:
        const = ctx.enter_context(tc.tile_pool(name="const", bufs=1))
        h_raw_pool = ctx.enter_context(tc.tile_pool(name="h_raw", bufs=3))
        h_grp_pool = ctx.enter_context(tc.tile_pool(name="h_grp", bufs=4))
        w_raw_pool = ctx.enter_context(tc.tile_pool(name="w_raw", bufs=16))
        w_grp_pool = ctx.enter_context(tc.tile_pool(name="w_grp", bufs=6))
        w_mx_pool = ctx.enter_context(tc.tile_pool(name="w_mx", bufs=6))
        soft = ctx.enter_context(tc.tile_pool(name="soft", bufs=2))
        acc_pool = ctx.enter_context(tc.psum_pool(name="acc", bufs=1))
        bank_pool = ctx.enter_context(tc.psum_pool(name="bank", bufs=4))

        h_raw = {}

        def load_h1(first, n):
            raw = h_raw_pool.tile([P, ROW_TILES, n * K_PASS], BF16, name="h_raw")
            nc.sync.dma_start(
                out=raw[:],
                in_=h1[:, first * K_PASS : (first + n) * K_PASS].rearrange("(p r) k -> p r k", p=P),
            )
            for s in range(n):
                h_raw[first + s] = raw[:, :, s * K_PASS : (s + 1) * K_PASS]

        w_raw = {}

        def load_w2(g):
            w_raw[g] = w_raw_pool.tile([P, PACK, H2], BF16, name="w_raw")
            nc.sync.dma_start(
                out=w_raw[g][:],
                in_=W2[g * K_PASS : (g + 1) * K_PASS, :].rearrange("(p t) n -> p t n", p=P),
            )

        b3_square = const.tile([P, A], BF16)
        nc.vector.memset(b3_square[:], 0.0)
        load_h1(0, PERIOD_PASSES)
        x_sb = const.tile([P, ROW_TILES, A * G], BF16)
        nc.sync.dma_start(out=x_sb[:], in_=x.rearrange("(p r) c -> p r c", p=P))
        b2_rows = const.tile([H2_TILES, P], BF16)
        nc.sync.dma_start(out=b2_rows[:], in_=b2.rearrange("(j p) -> j p", p=P))
        nc.sync.dma_start(out=b3_square[0:1, :], in_=b3.unsqueeze(0))
        w3_raw = const.tile([P, PACK, A], BF16)
        nc.sync.dma_start(out=w3_raw[:], in_=W3.rearrange("(t p) a -> p t a", p=P))
        for g in range(PASSES):
            if (g + 2) % PERIOD_PASSES == 0 and g + 2 < PASSES:
                load_h1(g + 2, PERIOD_PASSES)
            load_w2(g)

        ident = const.tile([P, P], F32)
        make_identity(nc, ident[:])

        zero_col = const.tile([P, 1], F32)
        nc.vector.memset(zero_col[:], 0.0)
        one_col = const.tile([P, 1], F32)
        nc.scalar.activation(out=one_col[:], in_=zero_col[:], func=ACT.Exp)

        ones = const.tile([P, P], BF16)
        nc.vector.memset(ones[:], 1.0)
        b2_square = const.tile([P, P], F32)
        nc.vector.memset(b2_square[:], 0.0)

        h_codes = const.tile([P, PASSES * B], U32, align_bytes=64)
        h_scale = const.tile([P, PASSES * B], U8, align_bytes=64)
        acc = [acc_pool.tile([P, B], F32, name="acc%d" % j) for j in range(H2_TILES)]

        def transpose_h1(g):
            bank = bank_pool.tile([P, 2, B], F32, tag="bank", name="h_bank")
            for u in range(2):
                for r in range(ROW_TILES):
                    words = h_raw[g][:, r, :].bitcast(F32)
                    nc.tensor.transpose(bank[:, u, r * P : (r + 1) * P], words[:, u::2], ident[:])
            return bank

        h_grp = {}

        def copy_h1(g, bank):
            c, s = g // GROUP_PASSES, g % GROUP_PASSES
            if s == 0:
                h_grp[c] = h_grp_pool.tile(
                    [P, GROUP_PASSES * B * PACK], BF16, align_bytes=64, name="h_grp"
                )
            pairs = h_grp[c][:].bitcast(F32)[:, s * 2 * B : (s + 1) * 2 * B]
            nc.scalar.copy(
                out=pairs.rearrange("p (i u) -> p i u", u=2), in_=bank[:].rearrange("p u i -> p i u")
            )

        def quantise_h1(c):
            cols = slice(c * GROUP_PASSES * B, (c + 1) * GROUP_PASSES * B)
            nc.vector.quantize_mx(
                out=h_codes[:, cols].bitcast(FP8X4), scales=h_scale[:, cols], in_=h_grp[c][:]
            )

        def regroup_w2(g):
            rows = w_raw[g]
            cut = VECTOR_COLS if g + H1_AHEAD < PASSES else VECTOR_COLS_END
            grp = w_grp_pool.tile([P, H2, PACK], BF16, align_bytes=64, name="w_grp")
            nc.vector.tensor_copy(
                out=grp[:, 0:cut, :].rearrange("p (c i) t -> p c t i", i=RUN),
                in_=rows[:, :, 0:cut].rearrange("p t (c i) -> p c t i", i=RUN),
            )
            nc.scalar.copy(
                out=grp[:, cut:H2, :].rearrange("p (c i) t -> p c t i", i=RUN),
                in_=rows[:, :, cut:H2].rearrange("p t (c i) -> p c t i", i=RUN),
            )
            return grp

        def quantise_w2(grp, halves):
            codes = w_mx_pool.tile([P, H2], U32, align_bytes=64, name="w_codes")
            scale = w_mx_pool.tile([P, H2], U8, align_bytes=64, name="w_scale")
            for cols in halves:
                nc.vector.quantize_mx(
                    out=codes[:, cols].bitcast(FP8X4),
                    scales=scale[:, cols],
                    in_=grp[:, cols, :].rearrange("p n t -> p (n t)"),
                )
            return codes, scale

        def multiply(g, codes, scale):
            rows = slice(g * B, (g + 1) * B)
            for j in range(H2_TILES):
                cols = slice(j * P, (j + 1) * P)
                nc.tensor.matmul_mx(
                    out=acc[j][:],
                    lhsT=codes[:, cols].bitcast(FP8X4),
                    lhsT_scale=scale[:, cols],
                    rhs=h_codes[:, rows].bitcast(FP8X4),
                    rhs_scale=h_scale[:, rows],
                    start=(g == 0),
                    stop=(g == PASSES - 1),
                )

        banks = {}
        with tc.manual_schedule():
            for g in range(PERIOD_PASSES):
                banks[g] = transpose_h1(g)
            for g in range(PERIOD_PASSES):
                copy_h1(g, banks[g])
            for c in range(PERIOD_PASSES // GROUP_PASSES):
                quantise_h1(c)

        nc.vector.tensor_copy(out=b2_square[0:H2_TILES, :], in_=b2_rows[:])
        b2_bank = bank_pool.tile([P, P], F32, tag="bank")
        nc.tensor.transpose(b2_bank[:], b2_square[:], ident[:])
        b2_col = const.tile([P, H2_TILES], F32)
        nc.vector.tensor_copy(out=b2_col[:], in_=b2_bank[:, 0:H2_TILES])

        gsum = const.tile([P, ROW_TILES, A], F32)
        nc.vector.tensor_reduce(
            out=gsum[:], in_=x_sb[:].rearrange("p r (a g) -> p r a g", g=G), axis=AX.X, op=ALU.add
        )
        bias_mask = const.tile([P, ROW_TILES, A], F32)
        nc.vector.tensor_scalar(
            out=bias_mask[:], in0=gsum[:], scalar1=0.0, scalar2=MASKED, op0=ALU.is_equal, op1=ALU.mult
        )
        b3_bank = bank_pool.tile([P, A], F32, tag="bank")
        nc.tensor.matmul(b3_bank[:], lhsT=ones[:], rhs=b3_square[:], start=True, stop=True)
        for r in range(ROW_TILES):
            nc.vector.tensor_tensor(
                out=bias_mask[:, r, :], in0=b3_bank[:], in1=bias_mask[:, r, :], op=ALU.add
            )

        w3_grp = const.tile([P, A, PACK], BF16, align_bytes=64)
        nc.vector.tensor_copy(out=w3_grp[:], in_=w3_raw[:].rearrange("p t a -> p a t"))
        w3_codes = const.tile([P, A], U32, align_bytes=64)
        w3_scale = const.tile([P, A], U8, align_bytes=64)
        nc.vector.quantize_mx(
            out=w3_codes[:].bitcast(FP8X4),
            scales=w3_scale[:],
            in_=w3_grp[:].rearrange("p a t -> p (a t)"),
        )

        w_grp = {}
        w_mx = {}
        with tc.manual_schedule():
            for g in range(PASSES + 2):
                h = g + H1_AHEAD
                if PERIOD_PASSES <= h + 1 < PASSES:
                    banks[h + 1] = transpose_h1(h + 1)
                if PERIOD_PASSES <= h < PASSES:
                    copy_h1(h, banks[h])
                if g < PASSES:
                    w_grp[g] = regroup_w2(g)
                if 1 <= g <= PASSES:
                    parts = 2 if g == PASSES else 1
                    width = H2 // parts
                    w_mx[g - 1] = quantise_w2(
                        w_grp[g - 1], [slice(i * width, (i + 1) * width) for i in range(parts)]
                    )
                if PERIOD_PASSES <= h < PASSES and (h + 1) % GROUP_PASSES == 0:
                    quantise_h1(h // GROUP_PASSES)
                if g >= 2:
                    multiply(g - 2, w_mx[g - 2][0], w_mx[g - 2][1])

        pre = const.tile([P, H2_TILES, B], F32)
        for j in range(H2_TILES):
            if j % 2 == 0:
                nc.vector.tensor_scalar(
                    out=pre[:, j, :], in0=acc[j][:], scalar1=b2_col[:, j : j + 1], scalar2=None, op0=ALU.add
                )
            else:
                nc.scalar.activation(
                    out=pre[:, j, :], in_=acc[j][:], func=ACT.Identity, bias=b2_col[:, j : j + 1], scale=1.0
                )
        h2_grp = const.tile([P, B, PACK], BF16, align_bytes=64)
        h2_codes = const.tile([P, B], U32, align_bytes=64)
        h2_scale = const.tile([P, B], U8, align_bytes=64)
        for r in range(ROW_TILES):
            rows = slice(r * P, (r + 1) * P)
            turned = pre[:, :, rows].rearrange("p t i -> p i t")
            nc.vector.scalar_tensor_tensor(
                out=h2_grp[:, rows, :], in0=turned, scalar=SLOPE, in1=turned, op0=ALU.mult, op1=ALU.max
            )
        for r in range(ROW_TILES):
            rows = slice(r * P, (r + 1) * P)
            nc.vector.quantize_mx(
                out=h2_codes[:, rows].bitcast(FP8X4),
                scales=h2_scale[:, rows],
                in_=h2_grp[:, rows, :].rearrange("p i t -> p (i t)"),
            )

        logits, negated, neg_max, expd, row_sum, inv_sum = {}, {}, {}, {}, {}, {}
        for r in range(ROW_TILES):
            rows = slice(r * P, (r + 1) * P)
            logits[r] = bank_pool.tile([P, A], F32, tag="bank", name="logits")
            nc.tensor.matmul_mx(
                out=logits[r][:],
                lhsT=h2_codes[:, rows].bitcast(FP8X4),
                lhsT_scale=h2_scale[:, rows],
                rhs=w3_codes[:].bitcast(FP8X4),
                rhs_scale=w3_scale[:],
                start=True,
                stop=True,
            )
        with tc.manual_schedule():
            for r in range(ROW_TILES):
                negated[r] = soft.tile([P, A], F32, name="negated")
                nc.vector.scalar_tensor_tensor(
                    out=negated[r][:],
                    in0=logits[r][:],
                    scalar=-1.0,
                    in1=bias_mask[:, r, :],
                    op0=ALU.mult,
                    op1=ALU.subtract,
                )
            for r in range(ROW_TILES):
                neg_max[r] = soft.tile([P, 1], F32, name="neg_max")
                nc.vector.tensor_reduce(out=neg_max[r][:], in_=negated[r][:], axis=AX.X, op=ALU.min)
            for r in range(ROW_TILES):
                expd[r] = soft.tile([P, A], F32, name="expd")
                row_sum[r] = soft.tile([P, 1], F32, name="row_sum")
                nc.scalar.activation(
                    out=expd[r][:],
                    in_=negated[r][:],
                    func=ACT.Exp,
                    bias=neg_max[r][:],
                    scale=-1.0,
                    accum_out=row_sum[r][:],
                )
            for r in range(ROW_TILES):
                inv_sum[r] = soft.tile([P, 1], F32, name="inv_sum")
                nc.vector.reciprocal(out=inv_sum[r][:], in_=row_sum[r][:])
            for r in range(ROW_TILES):
                prob = soft.tile([P, A], F32, name="prob")
                nc.vector.tensor_scalar(
                    out=prob[:], in0=expd[r][:], scalar1=inv_sum[r][:], scalar2=None, op0=ALU.mult
                )
                nc.sync.dma_start(out=out.rearrange("(p r) a -> r p a", p=P)[r], in_=prob[:])
